import numpy as np
import ml_dtypes


def mxq(x, axis, fmt="e4m3"):
    dtype, down = {"e4m3": (ml_dtypes.float8_e4m3fn, 7), "e5m2": (ml_dtypes.float8_e5m2, 14)}[fmt]
    v = np.moveaxis(np.asarray(x, np.float32).astype(ml_dtypes.bfloat16).astype(np.float64), axis, -1)
    blocks = v.reshape(v.shape[:-1] + (-1, 32))
    amax = np.abs(blocks).max(-1, keepdims=True)
    byte = np.maximum(np.where(amax > 0, np.frexp(amax)[1] - 1 + 127, 0) - down, 1)
    scale = np.exp2(byte - 127.0)
    codes = (blocks / scale).astype(np.float32).astype(dtype).astype(np.float64)
    return np.moveaxis((codes * scale).reshape(v.shape), -1, axis)


WIDE = False


def mx_kscale(k):
    if not WIDE:
        return np.ones(k)
    levels = np.array([10, -10, 5, -5, 0])
    a = np.random.permutation(np.resize(levels, k // 512 * 4)).reshape(k // 512, 4)
    idx = np.arange(k)
    return np.exp2(a[idx // 512, idx % 128 // 32])


BF16 = ml_dtypes.bfloat16


def bf(x):
    return np.asarray(x, np.float32).astype(BF16)


def f64(x):
    return np.asarray(x).astype(np.float64)


E2M1 = np.array([0.0, 0.5, 1.0, 1.5, 2.0, 3.0, 4.0, 6.0, -0.0, -0.5, -1.0, -1.5, -2.0, -3.0, -4.0, -6.0])


def pack_weight(w, fmt):
    k, n = w.shape
    w = f64(bf(w)).reshape(k // 32, 32, n)
    amax = np.abs(w).max(1)
    if fmt == "e4m3":
        byte = np.frexp(amax)[1] - 1 + 127 - 7
    else:
        mant, ex = np.frexp(amax / 6.0)
        byte = np.where(mant > 0.5, ex, ex - 1) + 127
    byte = np.clip(np.where(amax > 0, byte, 1), 1, 254)
    scaled = (w * np.exp2(127.0 - byte)[:, None, :]).reshape(k, n).astype(np.float32)
    by_word = np.ascontiguousarray(scaled.reshape(k // 512, 128, 4, n).transpose(0, 1, 3, 2))
    if fmt == "e4m3":
        words = by_word.astype(ml_dtypes.float8_e4m3fn).view(np.uint8)
    else:
        c = by_word.astype(ml_dtypes.float4_e2m1fn).view(np.uint8) & 0xF
        words = c[..., 0::2] | (c[..., 1::2] << 4)
    return np.ascontiguousarray(words), np.ascontiguousarray(byte.astype(np.uint8).reshape(k // 512, 16, n))


def unpack_weight(words, scales, fmt):
    g, p, n, _ = words.shape
    if fmt == "e4m3":
        vals = np.ascontiguousarray(words).view(ml_dtypes.float8_e4m3fn).astype(np.float64)
    else:
        nib = np.empty((g, p, n, 4), np.uint8)
        nib[..., 0::2] = words & 0xF
        nib[..., 1::2] = words >> 4
        vals = E2M1[nib]
    vals = vals * np.repeat(np.exp2(scales.astype(np.float64) - 127.0), 8, axis=1)[..., None]
    return vals.transpose(0, 1, 3, 2).reshape(g * 512, n)

def pack4(w):
    words, scales = pack_weight(w, "e2m1")
    return words.reshape(words.shape[0], 128, -1), scales


def unpack4(words, scales):
    return unpack_weight(words.reshape(words.shape[0], 128, -1, 2), scales, "e2m1")


B, S, IN, OUT, A, R = 8, 128, 2048, 2048, 8, 128
G = B // A
SCALING = 2.0


def setup_inputs():
    s = mx_kscale(IN)
    data = bf(np.random.standard_normal((B, S, IN)) * s)
    w = np.random.standard_normal((OUT, IN)) / np.sqrt(IN) / s
    W_words, W_scales = pack4(np.ascontiguousarray(w.T))
    t_lora = bf(np.random.standard_normal((A, G, S, R)))
    lora_b = bf(np.random.standard_normal((A, OUT, R)) * 0.5 / np.sqrt(R))
    return {"data": data,
            "W_words": W_words,
            "W_scales": W_scales,
            "t_lora": t_lora,
            "lora_b": lora_b}


def reference(data, W_words, W_scales, t_lora, lora_b):
    base = mxq(f64(data), 2, "e4m3") @ unpack4(W_words, W_scales)
    delta = (f64(t_lora).reshape(A, G * S, R) @ f64(lora_b).transpose(0, 2, 1)) * SCALING
    return base + delta.reshape(B, S, OUT)

@@ -1,0 +1,200 @@
+from contextlib import ExitStack
+
+import concourse.mybir as mybir
+from concourse.masks import make_identity
+
+F32 = mybir.dt.float32
+BF16 = mybir.dt.bfloat16
+I32 = mybir.dt.int32
+U32 = mybir.dt.uint32
+U8 = mybir.dt.uint8
+FP8X4 = mybir.dt.float8_e4m3fn_x4
+FP4X4 = mybir.dt.float4_e2m1fn_x4
+
+P = 128
+PACK = 4
+K_PASS = P * PACK
+ROWS = 8
+IN = 2048
+OUT = 2048
+PASSES = IN // K_PASS
+N_CHUNK = 512
+CHUNKS = OUT // N_CHUNK
+SCALING = 2.0
+LEAD = 4
+
+FLOPS = 2 * ROWS * P * OUT * (IN + P)
+
+
+def tile_linear_pa_kernel(tc, data, W_words, W_scales, t_lora, lora_b, out):
+    nc = tc.nc
+    with ExitStack() as ctx:
+        const = ctx.enter_context(tc.tile_pool(name="const", bufs=1))
+        per_row = ctx.enter_context(tc.tile_pool(name="per_row", bufs=ROWS))
+        work = ctx.enter_context(tc.tile_pool(name="work", bufs=2))
+        psum_bT = ctx.enter_context(tc.psum_pool(name="psum_bT", bufs=2))
+        psum_xT = ctx.enter_context(tc.psum_pool(name="psum_xT", bufs=2))
+        psum_acc = ctx.enter_context(tc.psum_pool(name="psum_acc", bufs=4))
+        ctx.enter_context(tc.manual_schedule())
+
+        ident_f32 = const.tile([P, P], F32)
+        make_identity(nc, ident_f32[:])
+        ident_bf16 = const.tile([P, P], BF16)
+        make_identity(nc, ident_bf16[:])
+
+        w_planes = const.tile([P, PASSES, OUT], U8, align_bytes=64)
+        nc.vector.memset(w_planes[:].bitcast(I32), 0)
+
+        w_words = const.tile([P, CHUNKS, PASSES, 2 * N_CHUNK], U8, align_bytes=64)
+        t_sb = const.tile([P, ROWS, P], BF16)
+        lb_tiles = []
+        x_tiles = []
+
+        def load_lora_b(row):
+            lb = per_row.tile([P, CHUNKS, PACK, P], BF16)
+            nc.sync.dma_start(
+                out=lb[:].rearrange("p c j r -> p c (j r)"),
+                in_=lora_b[row].rearrange("(c p j) r -> p c (j r)", c=CHUNKS, p=P, j=PACK),
+            )
+            lb_tiles.append(lb)
+
+        def load_x(row):
+            x_sb = per_row.tile([P, IN], BF16)
+            nc.sync.dma_start(out=x_sb[:], in_=data[row])
+            x_tiles.append(x_sb)
+
+        def load_w():
+            for q in range(8):
+                partition = 32 * (q // 4) + q % 4
+                nc.sync.dma_start(
+                    out=w_planes[partition:P:64, :, :].bitcast(I32),
+                    in_=W_scales[:, q:16:8, :].bitcast(I32).rearrange("g q n -> q g n"),
+                )
+            for n in range(CHUNKS):
+                nc.sync.dma_start(
+                    out=w_words[:, n, :, :].bitcast(I32),
+                    in_=W_words[:, :, 2 * N_CHUNK * n : 2 * N_CHUNK * (n + 1)]
+                    .bitcast(I32)
+                    .rearrange("g p b -> p g b"),
+                )
+
+        load_lora_b(0)
+        nc.sync.dma_start(out=t_sb[:], in_=t_lora.rearrange("a g s r -> s (a g) r"))
+        for step in range(ROWS + LEAD):
+            if step + 1 < ROWS:
+                load_lora_b(step + 1)
+            if 0 <= step - LEAD + 1 < ROWS:
+                load_x(step - LEAD + 1)
+            if step == LEAD:
+                load_w()
+
+        bT_tiles = {}
+        out_tiles = {}
+        x_mx = {}
+
+        def transpose_lora_b(row):
+            bT = work.tile([P, CHUNKS, N_CHUNK], BF16)
+            for half in range(2):
+                bT_ps = psum_bT.tile([P, 2, PACK, P], BF16, tag="bT_ps")
+                for c in range(2):
+                    for j in range(PACK):
+                        nc.tensor.transpose(
+                            out=bT_ps[:, c, j, :],
+                            in_=lb_tiles[row][:, 2 * half + c, j, :],
+                            identity=ident_bf16[:],
+                        )
+                nc.scalar.copy(
+                    out=bT[:, 2 * half : 2 * half + 2, :],
+                    in_=bT_ps[:].rearrange("r c j p -> r c (j p)"),
+                )
+            bT_tiles[row] = bT
+
+        def transpose_x(row):
+            x_words = x_tiles[row][:].bitcast(F32)
+            grouped = work.tile([P, PASSES, P, PACK], BF16, align_bytes=64)
+            for half in range(2):
+                xT_ps = psum_xT.tile([P, 2, 2, P], F32)
+                for g in range(2):
+                    word = (K_PASS // 2) * (2 * half + g)
+                    for u in range(2):
+                        nc.tensor.transpose(
+                            out=xT_ps[:, g, u, :],
+                            in_=x_words[:, word + u : word + K_PASS // 2 : 2],
+                            identity=ident_f32[:],
+                        )
+                nc.scalar.copy(
+                    out=grouped[:].bitcast(F32)[:, 2 * half : 2 * half + 2, :, :],
+                    in_=xT_ps[:].rearrange("p g u s -> p g s u"),
+                )
+            return grouped
+
+        def quantise_x(row, grouped):
+            codes = work.tile([P, PASSES, P], U32, align_bytes=64)
+            scales = work.tile([P, PASSES, P], U8, align_bytes=64)
+            nc.vector.quantize_mx(
+                out=codes[:].rearrange("p g s -> p (g s)").bitcast(FP8X4),
+                scales=scales[:].rearrange("p g s -> p (g s)"),
+                in_=grouped[:].rearrange("p g s t -> p (g s t)"),
+            )
+            x_mx[row] = (codes, scales)
+
+        def low_rank_chunk(row, c):
+            acc = psum_acc.tile([P, N_CHUNK], F32, tag="acc")
+            nc.tensor.matmul(
+                out=acc[:], lhsT=tT[:, row, :], rhs=bT_tiles[row][:, c, :], start=True, stop=True
+            )
+            dst = out_tiles[row][:, N_CHUNK * c : N_CHUNK * (c + 1)]
+            dst = dst.rearrange("s (p j) -> s p j", j=PACK)
+            src = acc[:].rearrange("s (j p) -> s p j", j=PACK)
+            if c % 2 == 0:
+                nc.scalar.activation(
+                    out=dst, in_=src, func=mybir.ActivationFunctionType.Copy, scale=SCALING
+                )
+            else:
+                nc.vector.tensor_scalar(
+                    out=dst, in0=src, scalar1=SCALING, scalar2=None, op0=mybir.AluOpType.mult
+                )
+
+        def mx_chunk(row, n):
+            codes, scales = x_mx[row]
+            cols = slice(N_CHUNK * n, N_CHUNK * (n + 1))
+            acc = psum_acc.tile([P, N_CHUNK], F32, tag="acc")
+            for g in range(PASSES):
+                nc.tensor.matmul_mx(
+                    out=acc[:],
+                    lhsT=codes[:, g, :].bitcast(FP8X4),
+                    lhsT_scale=scales[:, g, :],
+                    rhs=w_words[:, n, g, :].bitcast(FP4X4),
+                    rhs_scale=w_planes[:, g, cols],
+                    start=(g == 0),
+                    stop=(g == PASSES - 1),
+                )
+            result = out_tiles[row][:, cols]
+            nc.vector.tensor_tensor(out=result, in0=acc[:], in1=result, op=mybir.AluOpType.add)
+            nc.sync.dma_start(out=out[row, :, cols], in_=result)
+
+        transpose_lora_b(0)
+        tT_ps = psum_bT.tile([P, ROWS, P], BF16, tag="bT_ps")
+        for row in range(ROWS):
+            nc.tensor.transpose(out=tT_ps[:, row, :], in_=t_sb[:, row, :], identity=ident_bf16[:])
+        tT = const.tile([P, ROWS, P], BF16)
+        nc.scalar.copy(out=tT[:], in_=tT_ps[:])
+
+        for step in range(ROWS + LEAD):
+            low_rank_row = step
+            mx_row = step - LEAD
+            x_row = mx_row + 1
+            if low_rank_row + 1 < ROWS:
+                transpose_lora_b(low_rank_row + 1)
+            if 0 <= x_row < ROWS:
+                grouped = transpose_x(x_row)
+            if low_rank_row < ROWS:
+                out_sb = per_row.tile([P, OUT], F32)
+                out_tiles[low_rank_row] = out_sb
+            for chunk in range(CHUNKS):
+                if mx_row >= 0:
+                    mx_chunk(mx_row, chunk)
+                if low_rank_row < ROWS:
+                    low_rank_chunk(low_rank_row, chunk)
+            if 0 <= x_row < ROWS:
+                quantise_x(x_row, grouped)

@@ -44,6 +44,12 @@ def tile_linear_pa_kernel(tc, data, W_words, W_scales, t_lora, lora_b, out):
 
         w_planes = const.tile([P, PASSES, OUT], U8, align_bytes=64)
         nc.vector.memset(w_planes[:].bitcast(I32), 0)
+        for q in range(8):
+            partition = 32 * (q // 4) + q % 4
+            nc.gpsimd.dma_start(
+                out=w_planes[partition:P:64, :, :].bitcast(F32),
+                in_=W_scales[:, q:16:8, :].bitcast(F32).rearrange("g q n -> q g n"),
+            )
 
         w_words = const.tile([P, CHUNKS, PASSES, 2 * N_CHUNK], U8, align_bytes=64)
         t_sb = const.tile([P, ROWS, P], BF16)
@@ -63,13 +69,7 @@ def tile_linear_pa_kernel(tc, data, W_words, W_scales, t_lora, lora_b, out):
             nc.sync.dma_start(out=x_sb[:], in_=data[row])
             x_tiles.append(x_sb)
 
-        def load_w():
-            for q in range(8):
-                partition = 32 * (q // 4) + q % 4
-                nc.sync.dma_start(
-                    out=w_planes[partition:P:64, :, :].bitcast(I32),
-                    in_=W_scales[:, q:16:8, :].bitcast(I32).rearrange("g q n -> q g n"),
-                )
+        def load_w_words():
             for n in range(CHUNKS):
                 nc.sync.dma_start(
                     out=w_words[:, n, :, :].bitcast(I32),
@@ -86,7 +86,7 @@ def tile_linear_pa_kernel(tc, data, W_words, W_scales, t_lora, lora_b, out):
             if 0 <= step - LEAD + 1 < ROWS:
                 load_x(step - LEAD + 1)
             if step == LEAD:
-                load_w()
+                load_w_words()
 
         bT_tiles = {}
         out_tiles = {}
@@ -103,7 +103,8 @@ def tile_linear_pa_kernel(tc, data, W_words, W_scales, t_lora, lora_b, out):
                             in_=lb_tiles[row][:, 2 * half + c, j, :],
                             identity=ident_bf16[:],
                         )
-                nc.scalar.copy(
+                copy_out = nc.scalar.copy if half == 0 else nc.vector.tensor_copy
+                copy_out(
                     out=bT[:, 2 * half : 2 * half + 2, :],
                     in_=bT_ps[:].rearrange("r c j p -> r c (j p)"),
                 )
@@ -187,7 +188,7 @@ def tile_linear_pa_kernel(tc, data, W_words, W_scales, t_lora, lora_b, out):
             if low_rank_row + 1 < ROWS:
                 transpose_lora_b(low_rank_row + 1)
             if 0 <= x_row < ROWS:
-                grouped = transpose_x(x_row)
+                quantise_x(x_row, transpose_x(x_row))
             if low_rank_row < ROWS:
                 out_sb = per_row.tile([P, OUT], F32)
                 out_tiles[low_rank_row] = out_sb
@@ -196,5 +197,3 @@ def tile_linear_pa_kernel(tc, data, W_words, W_scales, t_lora, lora_b, out):
                     mx_chunk(mx_row, chunk)
                 if low_rank_row < ROWS:
                     low_rank_chunk(low_rank_row, chunk)
-            if 0 <= x_row < ROWS:
-                quantise_x(x_row, grouped)

@@ -83,12 +83,13 @@ def tile_linear_pa_kernel(tc, data, W_words, W_scales, t_lora, lora_b, out):
         for step in range(ROWS + LEAD):
             if step + 1 < ROWS:
                 load_lora_b(step + 1)
-            if 0 <= step - LEAD + 1 < ROWS:
-                load_x(step - LEAD + 1)
+            if 0 <= step - LEAD + 2 < ROWS:
+                load_x(step - LEAD + 2)
             if step == LEAD:
                 load_w_words()
 
         bT_tiles = {}
+        sorted_tiles = {}
         out_tiles = {}
         x_mx = {}
 
@@ -110,17 +111,23 @@ def tile_linear_pa_kernel(tc, data, W_words, W_scales, t_lora, lora_b, out):
                 )
             bT_tiles[row] = bT
 
+        def sort_x(row):
+            x_sorted = work.tile([P, PASSES, 2, P], F32)
+            nc.scalar.copy(
+                out=x_sorted[:],
+                in_=x_tiles[row][:].bitcast(F32).rearrange("s (g p u) -> s g u p", g=PASSES, u=2),
+            )
+            sorted_tiles[row] = x_sorted
+
         def transpose_x(row):
-            x_words = x_tiles[row][:].bitcast(F32)
             grouped = work.tile([P, PASSES, P, PACK], BF16, align_bytes=64)
             for half in range(2):
                 xT_ps = psum_xT.tile([P, 2, 2, P], F32)
                 for g in range(2):
-                    word = (K_PASS // 2) * (2 * half + g)
                     for u in range(2):
                         nc.tensor.transpose(
                             out=xT_ps[:, g, u, :],
-                            in_=x_words[:, word + u : word + K_PASS // 2 : 2],
+                            in_=sorted_tiles[row][:, 2 * half + g, u, :],
                             identity=ident_f32[:],
                         )
                 nc.scalar.copy(
@@ -192,8 +199,13 @@ def tile_linear_pa_kernel(tc, data, W_words, W_scales, t_lora, lora_b, out):
             if low_rank_row < ROWS:
                 out_sb = per_row.tile([P, OUT], F32)
                 out_tiles[low_rank_row] = out_sb
-            for chunk in range(CHUNKS):
-                if mx_row >= 0:
+                for chunk in range(CHUNKS // 2):
+                    low_rank_chunk(low_rank_row, chunk)
+            if 0 <= x_row + 1 < ROWS:
+                sort_x(x_row + 1)
+            if mx_row >= 0:
+                for chunk in range(CHUNKS):
                     mx_chunk(mx_row, chunk)
-                if low_rank_row < ROWS:
+            if low_rank_row < ROWS:
+                for chunk in range(CHUNKS // 2, CHUNKS):
                     low_rank_chunk(low_rank_row, chunk)

@@ -22,6 +22,7 @@ N_CHUNK = 512
 CHUNKS = OUT // N_CHUNK
 SCALING = 2.0
 LEAD = 4
+WARMUP = 6
 
 FLOPS = 2 * ROWS * P * OUT * (IN + P)
 
@@ -42,13 +43,18 @@ def tile_linear_pa_kernel(tc, data, W_words, W_scales, t_lora, lora_b, out):
         ident_bf16 = const.tile([P, P], BF16)
         make_identity(nc, ident_bf16[:])
 
+        zeros = const.tile([P, N_CHUNK], BF16)
+        nc.vector.memset(zeros[:], 0.0)
+        warm_ps = psum_acc.tile([P, N_CHUNK], F32, tag="acc")
+        for repeat in range(WARMUP):
+            nc.tensor.matmul(out=warm_ps[:], lhsT=zeros[:, :P], rhs=zeros[:], start=True, stop=True)
+
         w_planes = const.tile([P, PASSES, OUT], U8, align_bytes=64)
         nc.vector.memset(w_planes[:].bitcast(I32), 0)
-        for q in range(8):
-            partition = 32 * (q // 4) + q % 4
+        for r in range(4):
             nc.gpsimd.dma_start(
-                out=w_planes[partition:P:64, :, :].bitcast(F32),
-                in_=W_scales[:, q:16:8, :].bitcast(F32).rearrange("g q n -> q g n"),
+                out=w_planes[r:P:32, :, :].bitcast(F32),
+                in_=W_scales[:, r:16:4, :].bitcast(F32).rearrange("g q n -> q g n"),
             )
 
         w_words = const.tile([P, CHUNKS, PASSES, 2 * N_CHUNK], U8, align_bytes=64)
@@ -58,10 +64,13 @@ def tile_linear_pa_kernel(tc, data, W_words, W_scales, t_lora, lora_b, out):
 
         def load_lora_b(row):
             lb = per_row.tile([P, CHUNKS, PACK, P], BF16)
-            nc.sync.dma_start(
-                out=lb[:].rearrange("p c j r -> p c (j r)"),
-                in_=lora_b[row].rearrange("(c p j) r -> p c (j r)", c=CHUNKS, p=P, j=PACK),
-            )
+            rows_of_p = lora_b[row].rearrange("(c p j) r -> p c (j r)", c=CHUNKS, p=P, j=PACK)
+            for half in range(2):
+                chunks = slice(2 * half, 2 * half + 2)
+                nc.sync.dma_start(
+                    out=lb[:, chunks, :, :].rearrange("p c j r -> p c (j r)"),
+                    in_=rows_of_p[:, chunks, :],
+                )
             lb_tiles.append(lb)
 
         def load_x(row):
@@ -78,9 +87,10 @@ def tile_linear_pa_kernel(tc, data, W_words, W_scales, t_lora, lora_b, out):
                     .rearrange("g p b -> p g b"),
                 )
 
-        load_lora_b(0)
         nc.sync.dma_start(out=t_sb[:], in_=t_lora.rearrange("a g s r -> s (a g) r"))
-        for step in range(ROWS + LEAD):
+        load_lora_b(0)
+        load_lora_b(1)
+        for step in range(1, ROWS + LEAD):
             if step + 1 < ROWS:
                 load_lora_b(step + 1)
             if 0 <= step - LEAD + 2 < ROWS:
@@ -130,7 +140,8 @@ def tile_linear_pa_kernel(tc, data, W_words, W_scales, t_lora, lora_b, out):
                             in_=sorted_tiles[row][:, 2 * half + g, u, :],
                             identity=ident_f32[:],
                         )
-                nc.scalar.copy(
+                copy_out = nc.scalar.copy if half == 0 else nc.vector.tensor_copy
+                copy_out(
                     out=grouped[:].bitcast(F32)[:, 2 * half : 2 * half + 2, :, :],
                     in_=xT_ps[:].rearrange("p g u s -> p g s u"),
                 )
@@ -181,14 +192,19 @@ def tile_linear_pa_kernel(tc, data, W_words, W_scales, t_lora, lora_b, out):
             nc.vector.tensor_tensor(out=result, in0=acc[:], in1=result, op=mybir.AluOpType.add)
             nc.sync.dma_start(out=out[row, :, cols], in_=result)
 
-        transpose_lora_b(0)
         tT_ps = psum_bT.tile([P, ROWS, P], BF16, tag="bT_ps")
         for row in range(ROWS):
             nc.tensor.transpose(out=tT_ps[:, row, :], in_=t_sb[:, row, :], identity=ident_bf16[:])
         tT = const.tile([P, ROWS, P], BF16)
         nc.scalar.copy(out=tT[:], in_=tT_ps[:])
+        transpose_lora_b(0)
+        out_sb = per_row.tile([P, OUT], F32)
+        out_tiles[0] = out_sb
+        for chunk in range(CHUNKS):
+            low_rank_chunk(0, chunk)
+        transpose_lora_b(1)
 
-        for step in range(ROWS + LEAD):
+        for step in range(1, ROWS + LEAD):
             low_rank_row = step
             mx_row = step - LEAD
             x_row = mx_row + 1

@@ -22,6 +22,7 @@ N_CHUNK = 512
 CHUNKS = OUT // N_CHUNK
 SCALING = 2.0
 LEAD = 4
+MM_N = 512
 WARMUP = 6
 
 FLOPS = 2 * ROWS * P * OUT * (IN + P)
@@ -102,24 +103,39 @@ def tile_linear_pa_kernel(tc, data, W_words, W_scales, t_lora, lora_b, out):
         sorted_tiles = {}
         out_tiles = {}
         x_mx = {}
+        grouped_tiles = {}
+
+        def lora_b_transposes(row):
+            bT = work.tile([P, CHUNKS, N_CHUNK], BF16)
+            bT_tiles[row] = bT
+            banks = {}
+
+            def one(half, c, j):
+                if c == 0 and j == 0:
+                    bT_ps = psum_bT.tile([P, 2, PACK, P], BF16, tag="bT_ps")
+                    banks[half] = bT_ps
+                nc.tensor.transpose(
+                    out=banks[half][:, c, j, :],
+                    in_=lb_tiles[row][:, 2 * half + c, j, :],
+                    identity=ident_bf16[:],
+                )
+                if c == 1 and j == PACK - 1:
+                    copy_out = nc.scalar.copy if half == 0 else nc.vector.tensor_copy
+                    copy_out(
+                        out=bT[:, 2 * half : 2 * half + 2, :],
+                        in_=banks[half][:].rearrange("r c j p -> r c (j p)"),
+                    )
+
+            return [
+                (lambda h=half, cc=c, jj=j: one(h, cc, jj))
+                for half in range(2)
+                for c in range(2)
+                for j in range(PACK)
+            ]
 
         def transpose_lora_b(row):
-            bT = work.tile([P, CHUNKS, N_CHUNK], BF16)
-            for half in range(2):
-                bT_ps = psum_bT.tile([P, 2, PACK, P], BF16, tag="bT_ps")
-                for c in range(2):
-                    for j in range(PACK):
-                        nc.tensor.transpose(
-                            out=bT_ps[:, c, j, :],
-                            in_=lb_tiles[row][:, 2 * half + c, j, :],
-                            identity=ident_bf16[:],
-                        )
-                copy_out = nc.scalar.copy if half == 0 else nc.vector.tensor_copy
-                copy_out(
-                    out=bT[:, 2 * half : 2 * half + 2, :],
-                    in_=bT_ps[:].rearrange("r c j p -> r c (j p)"),
-                )
-            bT_tiles[row] = bT
+            for call in lora_b_transposes(row):
+                call()
 
         def sort_x(row):
             x_sorted = work.tile([P, PASSES, 2, P], F32)
@@ -129,25 +145,36 @@ def tile_linear_pa_kernel(tc, data, W_words, W_scales, t_lora, lora_b, out):
             )
             sorted_tiles[row] = x_sorted
 
-        def transpose_x(row):
+        def x_transposes(row):
             grouped = work.tile([P, PASSES, P, PACK], BF16, align_bytes=64)
-            for half in range(2):
-                xT_ps = psum_xT.tile([P, 2, 2, P], F32)
-                for g in range(2):
-                    for u in range(2):
-                        nc.tensor.transpose(
-                            out=xT_ps[:, g, u, :],
-                            in_=sorted_tiles[row][:, 2 * half + g, u, :],
-                            identity=ident_f32[:],
-                        )
-                copy_out = nc.scalar.copy if half == 0 else nc.vector.tensor_copy
-                copy_out(
-                    out=grouped[:].bitcast(F32)[:, 2 * half : 2 * half + 2, :, :],
-                    in_=xT_ps[:].rearrange("p g u s -> p g s u"),
-                )
-            return grouped
+            grouped_tiles[row] = grouped
+            banks = {}
 
-        def quantise_x(row, grouped):
+            def one(half, g, u):
+                if g == 0 and u == 0:
+                    xT_ps = psum_xT.tile([P, 2, 2, P], F32)
+                    banks[half] = xT_ps
+                nc.tensor.transpose(
+                    out=banks[half][:, g, u, :],
+                    in_=sorted_tiles[row][:, 2 * half + g, u, :],
+                    identity=ident_f32[:],
+                )
+                if g == 1 and u == 1:
+                    copy_out = nc.scalar.copy if half == 0 else nc.vector.tensor_copy
+                    copy_out(
+                        out=grouped[:].bitcast(F32)[:, 2 * half : 2 * half + 2, :, :],
+                        in_=banks[half][:].rearrange("p g u s -> p g s u"),
+                    )
+
+            return [
+                (lambda h=half, gg=g, uu=u: one(h, gg, uu))
+                for half in range(2)
+                for g in range(2)
+                for u in range(2)
+            ]
+
+        def quantise_x(row):
+            grouped = grouped_tiles[row]
             codes = work.tile([P, PASSES, P], U32, align_bytes=64)
             scales = work.tile([P, PASSES, P], U8, align_bytes=64)
             nc.vector.quantize_mx(
@@ -157,22 +184,47 @@ def tile_linear_pa_kernel(tc, data, W_words, W_scales, t_lora, lora_b, out):
             )
             x_mx[row] = (codes, scales)
 
-        def low_rank_chunk(row, c):
-            acc = psum_acc.tile([P, N_CHUNK], F32, tag="acc")
-            nc.tensor.matmul(
-                out=acc[:], lhsT=tT[:, row, :], rhs=bT_tiles[row][:, c, :], start=True, stop=True
-            )
-            dst = out_tiles[row][:, N_CHUNK * c : N_CHUNK * (c + 1)]
-            dst = dst.rearrange("s (p j) -> s p j", j=PACK)
-            src = acc[:].rearrange("s (j p) -> s p j", j=PACK)
-            if c % 2 == 0:
-                nc.scalar.activation(
-                    out=dst, in_=src, func=mybir.ActivationFunctionType.Copy, scale=SCALING
+        def low_rank_matmuls(row):
+            banks = {}
+            parts = N_CHUNK // MM_N
+
+            def one(c, k):
+                if k == 0:
+                    acc = psum_acc.tile([P, N_CHUNK], F32, tag="acc")
+                    banks[c] = acc
+                acc = banks[c]
+                nc.tensor.matmul(
+                    out=acc[:, MM_N * k : MM_N * (k + 1)],
+                    lhsT=tT[:, row, :],
+                    rhs=bT_tiles[row][:, c, MM_N * k : MM_N * (k + 1)],
+                    start=True,
+                    stop=True,
                 )
-            else:
-                nc.vector.tensor_scalar(
-                    out=dst, in0=src, scalar1=SCALING, scalar2=None, op0=mybir.AluOpType.mult
-                )
+                if k == parts - 1:
+                    dst = out_tiles[row][:, N_CHUNK * c : N_CHUNK * (c + 1)]
+                    dst = dst.rearrange("s (p j) -> s p j", j=PACK)
+                    src = acc[:].rearrange("s (j p) -> s p j", j=PACK)
+                    if c % 2 == 0:
+                        nc.scalar.activation(
+                            out=dst, in_=src, func=mybir.ActivationFunctionType.Copy, scale=SCALING
+                        )
+                    else:
+                        nc.vector.tensor_scalar(
+                            out=dst, in0=src, scalar1=SCALING, scalar2=None, op0=mybir.AluOpType.mult
+                        )
+
+            return [(lambda cc=c, kk=k: one(cc, kk)) for c in range(CHUNKS) for k in range(parts)]
+
+        def weave(matmuls, transposes):
+            gaps = len(matmuls) - 1
+            done = 0
+            for k, call in enumerate(matmuls):
+                call()
+                if k < gaps:
+                    upto = (len(transposes) * (k + 1) + gaps - 1) // gaps
+                    for t_call in transposes[done:upto]:
+                        t_call()
+                    done = upto
 
         def mx_chunk(row, n):
             codes, scales = x_mx[row]
@@ -200,28 +252,30 @@ def tile_linear_pa_kernel(tc, data, W_words, W_scales, t_lora, lora_b, out):
         transpose_lora_b(0)
         out_sb = per_row.tile([P, OUT], F32)
         out_tiles[0] = out_sb
-        for chunk in range(CHUNKS):
-            low_rank_chunk(0, chunk)
+        for call in low_rank_matmuls(0):
+            call()
         transpose_lora_b(1)
 
         for step in range(1, ROWS + LEAD):
             low_rank_row = step
             mx_row = step - LEAD
             x_row = mx_row + 1
+            transposes = []
             if low_rank_row + 1 < ROWS:
-                transpose_lora_b(low_rank_row + 1)
+                transposes.extend(lora_b_transposes(low_rank_row + 1))
             if 0 <= x_row < ROWS:
-                quantise_x(x_row, transpose_x(x_row))
+                transposes.extend(x_transposes(x_row))
             if low_rank_row < ROWS:
                 out_sb = per_row.tile([P, OUT], F32)
                 out_tiles[low_rank_row] = out_sb
-                for chunk in range(CHUNKS // 2):
-                    low_rank_chunk(low_rank_row, chunk)
+                weave(low_rank_matmuls(low_rank_row), transposes)
+            else:
+                for call in transposes:
+                    call()
+            if 0 <= x_row < ROWS:
+                quantise_x(x_row)
             if 0 <= x_row + 1 < ROWS:
                 sort_x(x_row + 1)
             if mx_row >= 0:
                 for chunk in range(CHUNKS):
                     mx_chunk(mx_row, chunk)
-            if low_rank_row < ROWS:
-                for chunk in range(CHUNKS // 2, CHUNKS):
-                    low_rank_chunk(low_rank_row, chunk)

@@ -52,11 +52,6 @@ def tile_linear_pa_kernel(tc, data, W_words, W_scales, t_lora, lora_b, out):
 
         w_planes = const.tile([P, PASSES, OUT], U8, align_bytes=64)
         nc.vector.memset(w_planes[:].bitcast(I32), 0)
-        for r in range(4):
-            nc.gpsimd.dma_start(
-                out=w_planes[r:P:32, :, :].bitcast(F32),
-                in_=W_scales[:, r:16:4, :].bitcast(F32).rearrange("g q n -> q g n"),
-            )
 
         w_words = const.tile([P, CHUNKS, PASSES, 2 * N_CHUNK], U8, align_bytes=64)
         t_sb = const.tile([P, ROWS, P], BF16)
@@ -250,6 +245,12 @@ def tile_linear_pa_kernel(tc, data, W_words, W_scales, t_lora, lora_b, out):
         tT = const.tile([P, ROWS, P], BF16)
         nc.scalar.copy(out=tT[:], in_=tT_ps[:])
         transpose_lora_b(0)
+        nc.vector.memset(w_planes[:, 0, 0:64].bitcast(I32), 0)
+        for r in range(4):
+            nc.gpsimd.dma_start(
+                out=w_planes[r:P:32, :, :].bitcast(F32),
+                in_=W_scales[:, r:16:4, :].bitcast(F32).rearrange("g q n -> q g n"),
+            )
         out_sb = per_row.tile([P, OUT], F32)
         out_tiles[0] = out_sb
         for call in low_rank_matmuls(0):

@@ -23,7 +23,7 @@ CHUNKS = OUT // N_CHUNK
 SCALING = 2.0
 LEAD = 4
 MM_N = 512
-WARMUP = 6
+WARMUP = 4
 
 FLOPS = 2 * ROWS * P * OUT * (IN + P)
 
@@ -39,10 +39,10 @@ def tile_linear_pa_kernel(tc, data, W_words, W_scales, t_lora, lora_b, out):
         psum_acc = ctx.enter_context(tc.psum_pool(name="psum_acc", bufs=4))
         ctx.enter_context(tc.manual_schedule())
 
-        ident_f32 = const.tile([P, P], F32)
-        make_identity(nc, ident_f32[:])
         ident_bf16 = const.tile([P, P], BF16)
         make_identity(nc, ident_bf16[:])
+        ident_f32 = const.tile([P, P], F32)
+        make_identity(nc, ident_f32[:])
 
         zeros = const.tile([P, N_CHUNK], BF16)
         nc.vector.memset(zeros[:], 0.0)
@@ -58,16 +58,20 @@ def tile_linear_pa_kernel(tc, data, W_words, W_scales, t_lora, lora_b, out):
         lb_tiles = []
         x_tiles = []
 
-        def load_lora_b(row):
+        def load_lora_b(row, pieces):
             lb = per_row.tile([P, CHUNKS, PACK, P], BF16)
             rows_of_p = lora_b[row].rearrange("(c p j) r -> p c (j r)", c=CHUNKS, p=P, j=PACK)
-            for half in range(2):
-                chunks = slice(2 * half, 2 * half + 2)
+            lb_tiles.append(lb)
+            width = CHUNKS // pieces
+
+            def one(k):
+                chunks = slice(width * k, width * (k + 1))
                 nc.sync.dma_start(
                     out=lb[:, chunks, :, :].rearrange("p c j r -> p c (j r)"),
                     in_=rows_of_p[:, chunks, :],
                 )
-            lb_tiles.append(lb)
+
+            return [(lambda kk=k: one(kk)) for k in range(pieces)]
 
         def load_x(row):
             x_sb = per_row.tile([P, IN], BF16)
@@ -83,12 +87,20 @@ def tile_linear_pa_kernel(tc, data, W_words, W_scales, t_lora, lora_b, out):
                     .rearrange("g p b -> p g b"),
                 )
 
-        nc.sync.dma_start(out=t_sb[:], in_=t_lora.rearrange("a g s r -> s (a g) r"))
-        load_lora_b(0)
-        load_lora_b(1)
+        t_rows = t_lora.rearrange("a g s r -> s (a g) r")
+        first = load_lora_b(0, CHUNKS)
+        first[0]()
+        first[1]()
+        nc.sync.dma_start(out=t_sb[:, 0:1, :], in_=t_rows[:, 0:1, :])
+        first[2]()
+        first[3]()
+        nc.sync.dma_start(out=t_sb[:, 1:ROWS, :], in_=t_rows[:, 1:ROWS, :])
+        for call in load_lora_b(1, 2):
+            call()
         for step in range(1, ROWS + LEAD):
             if step + 1 < ROWS:
-                load_lora_b(step + 1)
+                for call in load_lora_b(step + 1, 2):
+                    call()
             if 0 <= step - LEAD + 2 < ROWS:
                 load_x(step - LEAD + 2)
             if step == LEAD:
@@ -147,7 +159,7 @@ def tile_linear_pa_kernel(tc, data, W_words, W_scales, t_lora, lora_b, out):
 
             def one(half, g, u):
                 if g == 0 and u == 0:
-                    xT_ps = psum_xT.tile([P, 2, 2, P], F32)
+                    xT_ps = psum_xT.tile([P, 2, 2, P], F32, tag="xT_ps")
                     banks[half] = xT_ps
                 nc.tensor.transpose(
                     out=banks[half][:, g, u, :],
@@ -239,12 +251,22 @@ def tile_linear_pa_kernel(tc, data, W_words, W_scales, t_lora, lora_b, out):
             nc.vector.tensor_tensor(out=result, in0=acc[:], in1=result, op=mybir.AluOpType.add)
             nc.sync.dma_start(out=out[row, :, cols], in_=result)
 
-        tT_ps = psum_bT.tile([P, ROWS, P], BF16, tag="bT_ps")
-        for row in range(ROWS):
-            nc.tensor.transpose(out=tT_ps[:, row, :], in_=t_sb[:, row, :], identity=ident_bf16[:])
         tT = const.tile([P, ROWS, P], BF16)
-        nc.scalar.copy(out=tT[:], in_=tT_ps[:])
-        transpose_lora_b(0)
+
+        def transpose_t(rows):
+            tT_ps = psum_xT.tile([P, ROWS, P], BF16, tag="xT_ps")
+            for row in rows:
+                nc.tensor.transpose(out=tT_ps[:, row, :], in_=t_sb[:, row, :], identity=ident_bf16[:])
+            nc.vector.tensor_copy(
+                out=tT[:, rows.start : rows.stop, :], in_=tT_ps[:, rows.start : rows.stop, :]
+            )
+
+        row0 = lora_b_transposes(0)
+        for call in row0[:8]:
+            call()
+        transpose_t(range(0, 1))
+        for call in row0[8:]:
+            call()
         nc.vector.memset(w_planes[:, 0, 0:64].bitcast(I32), 0)
         for r in range(4):
             nc.gpsimd.dma_start(
@@ -255,6 +277,7 @@ def tile_linear_pa_kernel(tc, data, W_words, W_scales, t_lora, lora_b, out):
         out_tiles[0] = out_sb
         for call in low_rank_matmuls(0):
             call()
+        transpose_t(range(1, ROWS))
         transpose_lora_b(1)
 
         for step in range(1, ROWS + LEAD):

@@ -21,7 +21,7 @@ PASSES = IN // K_PASS
 N_CHUNK = 512
 CHUNKS = OUT // N_CHUNK
 SCALING = 2.0
-LEAD = 4
+LEAD = 6
 MM_N = 512
 WARMUP = 4
 
@@ -101,10 +101,10 @@ def tile_linear_pa_kernel(tc, data, W_words, W_scales, t_lora, lora_b, out):
             if step + 1 < ROWS:
                 for call in load_lora_b(step + 1, 2):
                     call()
-            if 0 <= step - LEAD + 2 < ROWS:
-                load_x(step - LEAD + 2)
             if step == LEAD:
                 load_w_words()
+            if 0 <= step - LEAD + 2 < ROWS:
+                load_x(step - LEAD + 2)
 
         bT_tiles = {}
         sorted_tiles = {}

@@ -53,14 +53,14 @@ def tile_linear_pa_kernel(tc, data, W_words, W_scales, t_lora, lora_b, out):
         w_planes = const.tile([P, PASSES, OUT], U8, align_bytes=64)
         nc.vector.memset(w_planes[:].bitcast(I32), 0)
 
-        w_words = const.tile([P, CHUNKS, PASSES, 2 * N_CHUNK], U8, align_bytes=64)
+        w_words = const.tile([P, CHUNKS // 2, PASSES, 4 * N_CHUNK], U8, align_bytes=64)
         t_sb = const.tile([P, ROWS, P], BF16)
         lb_tiles = []
         x_tiles = []
 
         def load_lora_b(row, pieces):
             lb = per_row.tile([P, CHUNKS, PACK, P], BF16)
-            rows_of_p = lora_b[row].rearrange("(c p j) r -> p c (j r)", c=CHUNKS, p=P, j=PACK)
+            rows_of_p = lora_b[row].rearrange("(p c j) r -> p c (j r)", c=CHUNKS, p=P, j=PACK)
             lb_tiles.append(lb)
             width = CHUNKS // pieces
 
@@ -79,10 +79,10 @@ def tile_linear_pa_kernel(tc, data, W_words, W_scales, t_lora, lora_b, out):
             x_tiles.append(x_sb)
 
         def load_w_words():
-            for n in range(CHUNKS):
+            for h in range(CHUNKS // 2):
                 nc.sync.dma_start(
-                    out=w_words[:, n, :, :].bitcast(I32),
-                    in_=W_words[:, :, 2 * N_CHUNK * n : 2 * N_CHUNK * (n + 1)]
+                    out=w_words[:, h, :, :].bitcast(I32),
+                    in_=W_words[:, :, 4 * N_CHUNK * h : 4 * N_CHUNK * (h + 1)]
                     .bitcast(I32)
                     .rearrange("g p b -> p g b"),
                 )
@@ -95,11 +95,11 @@ def tile_linear_pa_kernel(tc, data, W_words, W_scales, t_lora, lora_b, out):
         first[2]()
         first[3]()
         nc.sync.dma_start(out=t_sb[:, 1:ROWS, :], in_=t_rows[:, 1:ROWS, :])
-        for call in load_lora_b(1, 2):
+        for call in load_lora_b(1, 1):
             call()
         for step in range(1, ROWS + LEAD):
             if step + 1 < ROWS:
-                for call in load_lora_b(step + 1, 2):
+                for call in load_lora_b(step + 1, 1):
                     call()
             if step == LEAD:
                 load_w_words()
@@ -208,8 +208,8 @@ def tile_linear_pa_kernel(tc, data, W_words, W_scales, t_lora, lora_b, out):
                     stop=True,
                 )
                 if k == parts - 1:
-                    dst = out_tiles[row][:, N_CHUNK * c : N_CHUNK * (c + 1)]
-                    dst = dst.rearrange("s (p j) -> s p j", j=PACK)
+                    dst = out_tiles[row][:].rearrange("s (p c j) -> s c p j", c=CHUNKS, j=PACK)
+                    dst = dst[:, c, :, :]
                     src = acc[:].rearrange("s (j p) -> s p j", j=PACK)
                     if c % 2 == 0:
                         nc.scalar.activation(
@@ -242,7 +242,9 @@ def tile_linear_pa_kernel(tc, data, W_words, W_scales, t_lora, lora_b, out):
                     out=acc[:],
                     lhsT=codes[:, g, :].bitcast(FP8X4),
                     lhsT_scale=scales[:, g, :],
-                    rhs=w_words[:, n, g, :].bitcast(FP4X4),
+                    rhs=w_words[
+                        :, n // 2, g, 2 * N_CHUNK * (n % 2) : 2 * N_CHUNK * (n % 2 + 1)
+                    ].bitcast(FP4X4),
                     rhs_scale=w_planes[:, g, cols],
                     start=(g == 0),
                     stop=(g == PASSES - 1),

@@ -298,10 +298,20 @@ def tile_linear_pa_kernel(tc, data, W_words, W_scales, t_lora, lora_b, out):
             else:
                 for call in transposes:
                     call()
-            if 0 <= x_row < ROWS:
+            if 0 <= x_row < ROWS and mx_row != 1:
                 quantise_x(x_row)
             if 0 <= x_row + 1 < ROWS:
                 sort_x(x_row + 1)
-            if mx_row >= 0:
+            if mx_row == 0:
+                for row in range(2):
+                    for chunk in range(CHUNKS // 2):
+                        mx_chunk(row, chunk)
+            elif mx_row == 1:
+                for row in range(2):
+                    for chunk in range(CHUNKS // 2, CHUNKS):
+                        mx_chunk(row, chunk)
+                    if row == 0:
+                        quantise_x(x_row)
+            elif mx_row >= 2:
                 for chunk in range(CHUNKS):
                     mx_chunk(mx_row, chunk)

@@ -23,6 +23,7 @@ CHUNKS = OUT // N_CHUNK
 SCALING = 2.0
 LEAD = 6
 MM_N = 512
+LAST_PIECES = 4
 WARMUP = 4
 
 FLOPS = 2 * ROWS * P * OUT * (IN + P)
@@ -146,7 +147,8 @@ def tile_linear_pa_kernel(tc, data, W_words, W_scales, t_lora, lora_b, out):
 
         def sort_x(row):
             x_sorted = work.tile([P, PASSES, 2, P], F32)
-            nc.scalar.copy(
+            copy_words = nc.vector.tensor_copy if row == 0 else nc.scalar.copy
+            copy_words(
                 out=x_sorted[:],
                 in_=x_tiles[row][:].bitcast(F32).rearrange("s (g p u) -> s g u p", g=PASSES, u=2),
             )
@@ -233,25 +235,27 @@ def tile_linear_pa_kernel(tc, data, W_words, W_scales, t_lora, lora_b, out):
                         t_call()
                     done = upto
 
-        def mx_chunk(row, n):
+        def mx_chunk(row, n, pieces=1):
             codes, scales = x_mx[row]
-            cols = slice(N_CHUNK * n, N_CHUNK * (n + 1))
-            acc = psum_acc.tile([P, N_CHUNK], F32, tag="acc")
-            for g in range(PASSES):
-                nc.tensor.matmul_mx(
-                    out=acc[:],
-                    lhsT=codes[:, g, :].bitcast(FP8X4),
-                    lhsT_scale=scales[:, g, :],
-                    rhs=w_words[
-                        :, n // 2, g, 2 * N_CHUNK * (n % 2) : 2 * N_CHUNK * (n % 2 + 1)
-                    ].bitcast(FP4X4),
-                    rhs_scale=w_planes[:, g, cols],
-                    start=(g == 0),
-                    stop=(g == PASSES - 1),
-                )
-            result = out_tiles[row][:, cols]
-            nc.vector.tensor_tensor(out=result, in0=acc[:], in1=result, op=mybir.AluOpType.add)
-            nc.sync.dma_start(out=out[row, :, cols], in_=result)
+            width = N_CHUNK // pieces
+            for piece in range(pieces):
+                first = N_CHUNK * n + width * piece
+                cols = slice(first, first + width)
+                in_half = first % (2 * N_CHUNK)
+                acc = psum_acc.tile([P, width], F32, tag="acc")
+                for g in range(PASSES):
+                    nc.tensor.matmul_mx(
+                        out=acc[:],
+                        lhsT=codes[:, g, :].bitcast(FP8X4),
+                        lhsT_scale=scales[:, g, :],
+                        rhs=w_words[:, n // 2, g, 2 * in_half : 2 * (in_half + width)].bitcast(FP4X4),
+                        rhs_scale=w_planes[:, g, cols],
+                        start=(g == 0),
+                        stop=(g == PASSES - 1),
+                    )
+                result = out_tiles[row][:, cols]
+                nc.vector.tensor_tensor(out=result, in0=acc[:], in1=result, op=mybir.AluOpType.add)
+                nc.sync.dma_start(out=out[row, :, cols], in_=result)
 
         tT = const.tile([P, ROWS, P], BF16)
 
@@ -314,4 +318,5 @@ def tile_linear_pa_kernel(tc, data, W_words, W_scales, t_lora, lora_b, out):
                         quantise_x(x_row)
             elif mx_row >= 2:
                 for chunk in range(CHUNKS):
-                    mx_chunk(mx_row, chunk)
+                    last = mx_row == ROWS - 1 and chunk == CHUNKS - 1
+                    mx_chunk(mx_row, chunk, LAST_PIECES if last else 1)

@@ -87,6 +87,14 @@ def tile_linear_pa_kernel(tc, data, W_words, W_scales, t_lora, lora_b, out):
                     .bitcast(I32)
                     .rearrange("g p b -> p g b"),
                 )
+                if h == 0:
+                    for r in range(4):
+                        nc.sync.dma_start(
+                            out=w_planes[r:P:32, :, OUT // 2 : OUT].bitcast(I32),
+                            in_=W_scales[:, r:16:4, OUT // 2 : OUT]
+                            .bitcast(I32)
+                            .rearrange("g q n -> q g n"),
+                        )
 
         t_rows = t_lora.rearrange("a g s r -> s (a g) r")
         first = load_lora_b(0, CHUNKS)
@@ -276,8 +284,8 @@ def tile_linear_pa_kernel(tc, data, W_words, W_scales, t_lora, lora_b, out):
         nc.vector.memset(w_planes[:, 0, 0:64].bitcast(I32), 0)
         for r in range(4):
             nc.gpsimd.dma_start(
-                out=w_planes[r:P:32, :, :].bitcast(F32),
-                in_=W_scales[:, r:16:4, :].bitcast(F32).rearrange("g q n -> q g n"),
+                out=w_planes[r:P:32, :, 0 : OUT // 2].bitcast(F32),
+                in_=W_scales[:, r:16:4, 0 : OUT // 2].bitcast(F32).rearrange("g q n -> q g n"),
             )
         out_sb = per_row.tile([P, OUT], F32)
         out_tiles[0] = out_sb

@@ -24,6 +24,7 @@ SCALING = 2.0
 LEAD = 6
 MM_N = 512
 LAST_PIECES = 4
+EARLY_T = 2
 WARMUP = 4
 
 FLOPS = 2 * ROWS * P * OUT * (IN + P)
@@ -100,16 +101,17 @@ def tile_linear_pa_kernel(tc, data, W_words, W_scales, t_lora, lora_b, out):
         first = load_lora_b(0, CHUNKS)
         first[0]()
         first[1]()
-        nc.sync.dma_start(out=t_sb[:, 0:1, :], in_=t_rows[:, 0:1, :])
+        nc.sync.dma_start(out=t_sb[:, 0:EARLY_T, :], in_=t_rows[:, 0:EARLY_T, :])
         first[2]()
         first[3]()
-        nc.sync.dma_start(out=t_sb[:, 1:ROWS, :], in_=t_rows[:, 1:ROWS, :])
         for call in load_lora_b(1, 1):
             call()
         for step in range(1, ROWS + LEAD):
             if step + 1 < ROWS:
                 for call in load_lora_b(step + 1, 1):
                     call()
+            if step == 1:
+                nc.sync.dma_start(out=t_sb[:, EARLY_T:ROWS, :], in_=t_rows[:, EARLY_T:ROWS, :])
             if step == LEAD:
                 load_w_words()
             if 0 <= step - LEAD + 2 < ROWS:
@@ -275,10 +277,13 @@ def tile_linear_pa_kernel(tc, data, W_words, W_scales, t_lora, lora_b, out):
                 out=tT[:, rows.start : rows.stop, :], in_=tT_ps[:, rows.start : rows.stop, :]
             )
 
+        def turn_late_t():
+            transpose_t(range(EARLY_T, ROWS))
+
         row0 = lora_b_transposes(0)
         for call in row0[:8]:
             call()
-        transpose_t(range(0, 1))
+        transpose_t(range(0, EARLY_T))
         for call in row0[8:]:
             call()
         nc.vector.memset(w_planes[:, 0, 0:64].bitcast(I32), 0)
@@ -291,7 +296,6 @@ def tile_linear_pa_kernel(tc, data, W_words, W_scales, t_lora, lora_b, out):
         out_tiles[0] = out_sb
         for call in low_rank_matmuls(0):
             call()
-        transpose_t(range(1, ROWS))
         transpose_lora_b(1)
 
         for step in range(1, ROWS + LEAD):
@@ -300,7 +304,10 @@ def tile_linear_pa_kernel(tc, data, W_words, W_scales, t_lora, lora_b, out):
             x_row = mx_row + 1
             transposes = []
             if low_rank_row + 1 < ROWS:
-                transposes.extend(lora_b_transposes(low_rank_row + 1))
+                calls = lora_b_transposes(low_rank_row + 1)
+                if step == 1:
+                    calls = calls[:6] + [turn_late_t] + calls[6:]
+                transposes.extend(calls)
             if 0 <= x_row < ROWS:
                 transposes.extend(x_transposes(x_row))
             if low_rank_row < ROWS:

from contextlib import ExitStack

import concourse.mybir as mybir
from concourse.masks import make_identity

F32 = mybir.dt.float32
BF16 = mybir.dt.bfloat16
I32 = mybir.dt.int32
U32 = mybir.dt.uint32
U8 = mybir.dt.uint8
FP8X4 = mybir.dt.float8_e4m3fn_x4
FP4X4 = mybir.dt.float4_e2m1fn_x4

P = 128
PACK = 4
K_PASS = P * PACK
ROWS = 8
IN = 2048
OUT = 2048
PASSES = IN // K_PASS
N_CHUNK = 512
CHUNKS = OUT // N_CHUNK
SCALING = 2.0
LEAD = 6
MM_N = 512
LAST_PIECES = 4
EARLY_T = 2
WARMUP = 4

FLOPS = 2 * ROWS * P * OUT * (IN + P)


def tile_linear_pa_kernel(tc, data, W_words, W_scales, t_lora, lora_b, out):
    nc = tc.nc
    with ExitStack() as ctx:
        const = ctx.enter_context(tc.tile_pool(name="const", bufs=1))
        per_row = ctx.enter_context(tc.tile_pool(name="per_row", bufs=ROWS))
        work = ctx.enter_context(tc.tile_pool(name="work", bufs=2))
        psum_bT = ctx.enter_context(tc.psum_pool(name="psum_bT", bufs=2))
        psum_xT = ctx.enter_context(tc.psum_pool(name="psum_xT", bufs=2))
        psum_acc = ctx.enter_context(tc.psum_pool(name="psum_acc", bufs=4))
        ctx.enter_context(tc.manual_schedule())

        ident_bf16 = const.tile([P, P], BF16)
        make_identity(nc, ident_bf16[:])
        ident_f32 = const.tile([P, P], F32)
        make_identity(nc, ident_f32[:])

        zeros = const.tile([P, N_CHUNK], BF16)
        nc.vector.memset(zeros[:], 0.0)
        warm_ps = psum_acc.tile([P, N_CHUNK], F32, tag="acc")
        for repeat in range(WARMUP):
            nc.tensor.matmul(out=warm_ps[:], lhsT=zeros[:, :P], rhs=zeros[:], start=True, stop=True)

        w_planes = const.tile([P, PASSES, OUT], U8, align_bytes=64)
        nc.vector.memset(w_planes[:].bitcast(I32), 0)

        w_words = const.tile([P, CHUNKS // 2, PASSES, 4 * N_CHUNK], U8, align_bytes=64)
        t_sb = const.tile([P, ROWS, P], BF16)
        lb_tiles = []
        x_tiles = []

        def load_lora_b(row, pieces):
            lb = per_row.tile([P, CHUNKS, PACK, P], BF16)
            rows_of_p = lora_b[row].rearrange("(p c j) r -> p c (j r)", c=CHUNKS, p=P, j=PACK)
            lb_tiles.append(lb)
            width = CHUNKS // pieces

            def one(k):
                chunks = slice(width * k, width * (k + 1))
                nc.sync.dma_start(
                    out=lb[:, chunks, :, :].rearrange("p c j r -> p c (j r)"),
                    in_=rows_of_p[:, chunks, :],
                )

            return [(lambda kk=k: one(kk)) for k in range(pieces)]

        def load_x(row):
            x_sb = per_row.tile([P, IN], BF16)
            nc.sync.dma_start(out=x_sb[:], in_=data[row])
            x_tiles.append(x_sb)

        def load_w_words():
            for h in range(CHUNKS // 2):
                nc.sync.dma_start(
                    out=w_words[:, h, :, :].bitcast(I32),
                    in_=W_words[:, :, 4 * N_CHUNK * h : 4 * N_CHUNK * (h + 1)]
                    .bitcast(I32)
                    .rearrange("g p b -> p g b"),
                )
                if h == 0:
                    for r in range(4):
                        nc.sync.dma_start(
                            out=w_planes[r:P:32, :, OUT // 2 : OUT].bitcast(I32),
                            in_=W_scales[:, r:16:4, OUT // 2 : OUT]
                            .bitcast(I32)
                            .rearrange("g q n -> q g n"),
                        )

        t_rows = t_lora.rearrange("a g s r -> s (a g) r")
        first = load_lora_b(0, CHUNKS)
        first[0]()
        first[1]()
        nc.sync.dma_start(out=t_sb[:, 0:EARLY_T, :], in_=t_rows[:, 0:EARLY_T, :])
        first[2]()
        first[3]()
        for call in load_lora_b(1, 1):
            call()
        for step in range(1, ROWS + LEAD):
            if step + 1 < ROWS:
                for call in load_lora_b(step + 1, 1):
                    call()
            if step == 1:
                nc.sync.dma_start(out=t_sb[:, EARLY_T:ROWS, :], in_=t_rows[:, EARLY_T:ROWS, :])
            if step == LEAD:
                load_w_words()
            if 0 <= step - LEAD + 2 < ROWS:
                load_x(step - LEAD + 2)

        bT_tiles = {}
        sorted_tiles = {}
        out_tiles = {}
        x_mx = {}
        grouped_tiles = {}

        def lora_b_transposes(row):
            bT = work.tile([P, CHUNKS, N_CHUNK], BF16)
            bT_tiles[row] = bT
            banks = {}

            def one(half, c, j):
                if c == 0 and j == 0:
                    bT_ps = psum_bT.tile([P, 2, PACK, P], BF16, tag="bT_ps")
                    banks[half] = bT_ps
                nc.tensor.transpose(
                    out=banks[half][:, c, j, :],
                    in_=lb_tiles[row][:, 2 * half + c, j, :],
                    identity=ident_bf16[:],
                )
                if c == 1 and j == PACK - 1:
                    copy_out = nc.scalar.copy if half == 0 else nc.vector.tensor_copy
                    copy_out(
                        out=bT[:, 2 * half : 2 * half + 2, :],
                        in_=banks[half][:].rearrange("r c j p -> r c (j p)"),
                    )

            return [
                (lambda h=half, cc=c, jj=j: one(h, cc, jj))
                for half in range(2)
                for c in range(2)
                for j in range(PACK)
            ]

        def transpose_lora_b(row):
            for call in lora_b_transposes(row):
                call()

        def sort_x(row):
            x_sorted = work.tile([P, PASSES, 2, P], F32)
            copy_words = nc.vector.tensor_copy if row == 0 else nc.scalar.copy
            copy_words(
                out=x_sorted[:],
                in_=x_tiles[row][:].bitcast(F32).rearrange("s (g p u) -> s g u p", g=PASSES, u=2),
            )
            sorted_tiles[row] = x_sorted

        def x_transposes(row):
            grouped = work.tile([P, PASSES, P, PACK], BF16, align_bytes=64)
            grouped_tiles[row] = grouped
            banks = {}

            def one(half, g, u):
                if g == 0 and u == 0:
                    xT_ps = psum_xT.tile([P, 2, 2, P], F32, tag="xT_ps")
                    banks[half] = xT_ps
                nc.tensor.transpose(
                    out=banks[half][:, g, u, :],
                    in_=sorted_tiles[row][:, 2 * half + g, u, :],
                    identity=ident_f32[:],
                )
                if g == 1 and u == 1:
                    copy_out = nc.scalar.copy if half == 0 else nc.vector.tensor_copy
                    copy_out(
                        out=grouped[:].bitcast(F32)[:, 2 * half : 2 * half + 2, :, :],
                        in_=banks[half][:].rearrange("p g u s -> p g s u"),
                    )

            return [
                (lambda h=half, gg=g, uu=u: one(h, gg, uu))
                for half in range(2)
                for g in range(2)
                for u in range(2)
            ]

        def quantise_x(row):
            grouped = grouped_tiles[row]
            codes = work.tile([P, PASSES, P], U32, align_bytes=64)
            scales = work.tile([P, PASSES, P], U8, align_bytes=64)
            nc.vector.quantize_mx(
                out=codes[:].rearrange("p g s -> p (g s)").bitcast(FP8X4),
                scales=scales[:].rearrange("p g s -> p (g s)"),
                in_=grouped[:].rearrange("p g s t -> p (g s t)"),
            )
            x_mx[row] = (codes, scales)

        def low_rank_matmuls(row):
            banks = {}
            parts = N_CHUNK // MM_N

            def one(c, k):
                if k == 0:
                    acc = psum_acc.tile([P, N_CHUNK], F32, tag="acc")
                    banks[c] = acc
                acc = banks[c]
                nc.tensor.matmul(
                    out=acc[:, MM_N * k : MM_N * (k + 1)],
                    lhsT=tT[:, row, :],
                    rhs=bT_tiles[row][:, c, MM_N * k : MM_N * (k + 1)],
                    start=True,
                    stop=True,
                )
                if k == parts - 1:
                    dst = out_tiles[row][:].rearrange("s (p c j) -> s c p j", c=CHUNKS, j=PACK)
                    dst = dst[:, c, :, :]
                    src = acc[:].rearrange("s (j p) -> s p j", j=PACK)
                    if c % 2 == 0:
                        nc.scalar.activation(
                            out=dst, in_=src, func=mybir.ActivationFunctionType.Copy, scale=SCALING
                        )
                    else:
                        nc.vector.tensor_scalar(
                            out=dst, in0=src, scalar1=SCALING, scalar2=None, op0=mybir.AluOpType.mult
                        )

            return [(lambda cc=c, kk=k: one(cc, kk)) for c in range(CHUNKS) for k in range(parts)]

        def weave(matmuls, transposes):
            gaps = len(matmuls) - 1
            done = 0
            for k, call in enumerate(matmuls):
                call()
                if k < gaps:
                    upto = (len(transposes) * (k + 1) + gaps - 1) // gaps
                    for t_call in transposes[done:upto]:
                        t_call()
                    done = upto

        def mx_chunk(row, n, pieces=1):
            codes, scales = x_mx[row]
            width = N_CHUNK // pieces
            for piece in range(pieces):
                first = N_CHUNK * n + width * piece
                cols = slice(first, first + width)
                in_half = first % (2 * N_CHUNK)
                acc = psum_acc.tile([P, width], F32, tag="acc")
                for g in range(PASSES):
                    nc.tensor.matmul_mx(
                        out=acc[:],
                        lhsT=codes[:, g, :].bitcast(FP8X4),
                        lhsT_scale=scales[:, g, :],
                        rhs=w_words[:, n // 2, g, 2 * in_half : 2 * (in_half + width)].bitcast(FP4X4),
                        rhs_scale=w_planes[:, g, cols],
                        start=(g == 0),
                        stop=(g == PASSES - 1),
                    )
                result = out_tiles[row][:, cols]
                nc.vector.tensor_tensor(out=result, in0=acc[:], in1=result, op=mybir.AluOpType.add)
                nc.sync.dma_start(out=out[row, :, cols], in_=result)

        tT = const.tile([P, ROWS, P], BF16)

        def transpose_t(rows):
            tT_ps = psum_xT.tile([P, ROWS, P], BF16, tag="xT_ps")
            for row in rows:
                nc.tensor.transpose(out=tT_ps[:, row, :], in_=t_sb[:, row, :], identity=ident_bf16[:])
            nc.vector.tensor_copy(
                out=tT[:, rows.start : rows.stop, :], in_=tT_ps[:, rows.start : rows.stop, :]
            )

        def turn_late_t():
            transpose_t(range(EARLY_T, ROWS))

        row0 = lora_b_transposes(0)
        for call in row0[:8]:
            call()
        transpose_t(range(0, EARLY_T))
        for call in row0[8:]:
            call()
        nc.vector.memset(w_planes[:, 0, 0:64].bitcast(I32), 0)
        for r in range(4):
            nc.gpsimd.dma_start(
                out=w_planes[r:P:32, :, 0 : OUT // 2].bitcast(F32),
                in_=W_scales[:, r:16:4, 0 : OUT // 2].bitcast(F32).rearrange("g q n -> q g n"),
            )
        out_sb = per_row.tile([P, OUT], F32)
        out_tiles[0] = out_sb
        for call in low_rank_matmuls(0):
            call()
        transpose_lora_b(1)

        for step in range(1, ROWS + LEAD):
            low_rank_row = step
            mx_row = step - LEAD
            x_row = mx_row + 1
            transposes = []
            if low_rank_row + 1 < ROWS:
                calls = lora_b_transposes(low_rank_row + 1)
                if step == 1:
                    calls = calls[:6] + [turn_late_t] + calls[6:]
                transposes.extend(calls)
            if 0 <= x_row < ROWS:
                transposes.extend(x_transposes(x_row))
            if low_rank_row < ROWS:
                out_sb = per_row.tile([P, OUT], F32)
                out_tiles[low_rank_row] = out_sb
                weave(low_rank_matmuls(low_rank_row), transposes)
            else:
                for call in transposes:
                    call()
            if 0 <= x_row < ROWS and mx_row != 1:
                quantise_x(x_row)
            if 0 <= x_row + 1 < ROWS:
                sort_x(x_row + 1)
            if mx_row == 0:
                for row in range(2):
                    for chunk in range(CHUNKS // 2):
                        mx_chunk(row, chunk)
            elif mx_row == 1:
                for row in range(2):
                    for chunk in range(CHUNKS // 2, CHUNKS):
                        mx_chunk(row, chunk)
                    if row == 0:
                        quantise_x(x_row)
            elif mx_row >= 2:
                for chunk in range(CHUNKS):
                    last = mx_row == ROWS - 1 and chunk == CHUNKS - 1
                    mx_chunk(mx_row, chunk, LAST_PIECES if last else 1)
